import numpy as np
import ml_dtypes


def mxq(x, axis, fmt="e4m3"):
    dtype, down = {"e4m3": (ml_dtypes.float8_e4m3fn, 7), "e5m2": (ml_dtypes.float8_e5m2, 14)}[fmt]
    v = np.moveaxis(np.asarray(x, np.float32).astype(ml_dtypes.bfloat16).astype(np.float64), axis, -1)
    blocks = v.reshape(v.shape[:-1] + (-1, 32))
    amax = np.abs(blocks).max(-1, keepdims=True)
    byte = np.maximum(np.where(amax > 0, np.frexp(amax)[1] - 1 + 127, 0) - down, 1)
    scale = np.exp2(byte - 127.0)
    codes = (blocks / scale).astype(np.float32).astype(dtype).astype(np.float64)
    return np.moveaxis((codes * scale).reshape(v.shape), -1, axis)


WIDE = False


def mx_kscale(k):
    if not WIDE:
        return np.ones(k)
    levels = np.array([10, -10, 5, -5, 0])
    a = np.random.permutation(np.resize(levels, k // 512 * 4)).reshape(k // 512, 4)
    idx = np.arange(k)
    return np.exp2(a[idx // 512, idx % 128 // 32])


BF16 = ml_dtypes.bfloat16


def bf(x):
    return np.asarray(x, np.float32).astype(BF16)


def f64(x):
    return np.asarray(x).astype(np.float64)


E2M1 = np.array([0.0, 0.5, 1.0, 1.5, 2.0, 3.0, 4.0, 6.0, -0.0, -0.5, -1.0, -1.5, -2.0, -3.0, -4.0, -6.0])


def pack_weight(w, fmt):
    k, n = w.shape
    w = f64(bf(w)).reshape(k // 32, 32, n)
    amax = np.abs(w).max(1)
    if fmt == "e4m3":
        byte = np.frexp(amax)[1] - 1 + 127 - 7
    else:
        mant, ex = np.frexp(amax / 6.0)
        byte = np.where(mant > 0.5, ex, ex - 1) + 127
    byte = np.clip(np.where(amax > 0, byte, 1), 1, 254)
    scaled = (w * np.exp2(127.0 - byte)[:, None, :]).reshape(k, n).astype(np.float32)
    by_word = np.ascontiguousarray(scaled.reshape(k // 512, 128, 4, n).transpose(0, 1, 3, 2))
    if fmt == "e4m3":
        words = by_word.astype(ml_dtypes.float8_e4m3fn).view(np.uint8)
    else:
        c = by_word.astype(ml_dtypes.float4_e2m1fn).view(np.uint8) & 0xF
        words = c[..., 0::2] | (c[..., 1::2] << 4)
    return np.ascontiguousarray(words), np.ascontiguousarray(byte.astype(np.uint8).reshape(k // 512, 16, n))


def unpack_weight(words, scales, fmt):
    g, p, n, _ = words.shape
    if fmt == "e4m3":
        vals = np.ascontiguousarray(words).view(ml_dtypes.float8_e4m3fn).astype(np.float64)
    else:
        nib = np.empty((g, p, n, 4), np.uint8)
        nib[..., 0::2] = words & 0xF
        nib[..., 1::2] = words >> 4
        vals = E2M1[nib]
    vals = vals * np.repeat(np.exp2(scales.astype(np.float64) - 127.0), 8, axis=1)[..., None]
    return vals.transpose(0, 1, 3, 2).reshape(g * 512, n)

def pack4(w):
    words, scales = pack_weight(w, "e2m1")
    return words.reshape(words.shape[0], 128, -1), scales


def unpack4(words, scales):
    return unpack_weight(words.reshape(words.shape[0], 128, -1, 2), scales, "e2m1")


B, D_IN, D_H = 128, 512, 1024


def sigmoid(v):
    return 1.0 / (1.0 + np.exp(-v))


def setup_inputs():
    s, t = mx_kscale(D_IN), mx_kscale(D_H)
    fg = np.exp(0.75 * np.random.standard_normal((B, D_H)))
    ig = np.exp(0.75 * np.random.standard_normal((B, D_H)))
    c = fg * np.random.standard_normal((B, D_H)) + ig * np.tanh(0.75 * np.random.standard_normal((B, D_H)))
    n = fg * np.random.uniform(size=(B, D_H)) + ig
    x = bf(np.random.standard_normal((B, D_IN)) * s)
    h_prev = bf(np.random.standard_normal((B, D_H)) * t)
    W_o_words, W_o_scales = pack4(np.random.standard_normal((D_IN, D_H)) * 0.5 / np.sqrt(D_IN) / s[:, None])
    b_o = bf(np.random.standard_normal(D_H) * 0.3)
    U_o_words, U_o_scales = pack4(np.random.standard_normal((D_H, D_H)) * 0.5 / np.sqrt(D_H) / t[:, None])
    return {"x": x,
            "h_prev": h_prev,
            "c": bf(c),
            "n": bf(n),
            "W_o_words": W_o_words,
            "W_o_scales": W_o_scales,
            "b_o": b_o,
            "U_o_words": U_o_words,
            "U_o_scales": U_o_scales}


def reference(x, h_prev, c, n, W_o_words, W_o_scales, b_o, U_o_words, U_o_scales):
    o = sigmoid((mxq(f64(x), 1, "e4m3") @ unpack4(W_o_words, W_o_scales)) + f64(b_o) + (mxq(f64(h_prev), 1, "e4m3") @ unpack4(U_o_words, U_o_scales)))
    return o * (f64(c) / (f64(n) + 1e-6))

@@ -1,0 +1,142 @@
+from contextlib import ExitStack
+
+import concourse.mybir as mybir
+from concourse.masks import make_identity
+
+F32 = mybir.dt.float32
+BF16 = mybir.dt.bfloat16
+I32 = mybir.dt.int32
+U8 = mybir.dt.uint8
+U32 = mybir.dt.uint32
+FP8X4 = mybir.dt.float8_e4m3fn_x4
+FP4X4 = mybir.dt.float4_e2m1fn_x4
+ACT = mybir.ActivationFunctionType
+ALU = mybir.AluOpType
+
+P = 128
+D_IN = 512
+D_H = 1024
+K_PASS = 512
+PASSES = (D_IN + D_H) // K_PASS
+BANK = 512
+BANKS = D_H // BANK
+EPS = 1e-6
+
+FLOPS = 2 * P * (D_IN + D_H) * D_H
+
+
+def load_scale_rows(nc, planes, scale_rows):
+    for r in range(4):
+        nc.sync.dma_start(
+            out=planes[r:P:32].bitcast(I32),
+            in_=scale_rows[:, r:16:4, :].rearrange("g q w -> q g w").bitcast(I32),
+        )
+
+
+def tile_slstmcell_pb_s_kernel(
+    tc, x, h_prev, c, n, W_o_words, W_o_scales, b_o, U_o_words, U_o_scales, out
+):
+    nc = tc.nc
+    with ExitStack() as stack:
+        sbuf = stack.enter_context(tc.tile_pool(name="sbuf", bufs=1))
+        psum = stack.enter_context(tc.psum_pool(name="psum", bufs=1))
+        stack.enter_context(tc.manual_schedule())
+        halves = [slice(k * BANK, (k + 1) * BANK) for k in range(BANKS)]
+
+        bias_rows = sbuf.tile([P, D_H], BF16)
+        nc.vector.memset(bias_rows[:].bitcast(I32), 0)
+        planes = sbuf.tile([P, PASSES, D_H], U8, align_bytes=64)
+        nc.vector.memset(planes[:].bitcast(I32), 0)
+        ones = sbuf.tile([P, P], BF16)
+        nc.vector.memset(ones[:], 1.0)
+        two_eps = sbuf.tile([P, 1], F32)
+        nc.vector.memset(two_eps[:], 2.0 * EPS)
+        ident = sbuf.tile([P, P], F32)
+        make_identity(nc, ident[:])
+
+        nc.scalar.dma_start(out=bias_rows[0:1, :], in_=b_o.rearrange("(o n) -> o n", o=1))
+        n_sb = sbuf.tile([P, D_H], BF16)
+        nc.sync.dma_start(out=n_sb[:], in_=n)
+        acts = sbuf.tile([P, PASSES, K_PASS], BF16)
+        nc.sync.dma_start(out=acts[:, 0, :], in_=x)
+        nc.sync.dma_start(out=acts[:, 1:3, :], in_=h_prev.rearrange("b (g k) -> b g k", g=2))
+        words = sbuf.tile([P, PASSES, 2 * D_H], U8, align_bytes=64)
+        load_scale_rows(nc, planes[:, 0:1, :], W_o_scales)
+        nc.sync.dma_start(out=words[:, 0, :].bitcast(I32), in_=W_o_words[0].bitcast(I32))
+        nc.sync.dma_start(out=words[:, 1, :].bitcast(I32), in_=U_o_words[0].bitcast(I32))
+        load_scale_rows(nc, planes[:, 1:3, :], U_o_scales)
+        nc.sync.dma_start(out=words[:, 2, :].bitcast(I32), in_=U_o_words[1].bitcast(I32))
+        c_sb = sbuf.tile([P, D_H], BF16)
+        nc.sync.dma_start(out=c_sb[:], in_=c)
+
+        log_2n = sbuf.tile([P, D_H], F32)
+        half_recip = sbuf.tile([P, D_H], F32)
+        for cols in halves:
+            nc.scalar.activation(out=log_2n[:, cols], in_=n_sb[:, cols], func=ACT.Ln, bias=two_eps[:, 0:1], scale=2.0)
+        for cols in halves:
+            nc.scalar.activation(out=half_recip[:, cols], in_=log_2n[:, cols], func=ACT.Exp, scale=-1.0)
+
+        flipped = []
+        for g in range(PASSES):
+            pair_words = acts[:, g, :].bitcast(F32)
+            flipped_g = psum.tile([P, 2, P], F32, name="flipped%d" % g)
+            for u in range(2):
+                nc.tensor.transpose(flipped_g[:, u, :], pair_words[:, u : K_PASS // 2 : 2], ident[:])
+            flipped.append(flipped_g)
+
+        bias_sb = sbuf.tile([P, D_H], F32)
+        bias_banks = []
+        for k in range(BANKS):
+            bias_ps = psum.tile([P, BANK], F32, name="bias_ps%d" % k)
+            nc.tensor.matmul(out=bias_ps[:], lhsT=ones[:], rhs=bias_rows[:, halves[k]], start=True, stop=True)
+            bias_banks.append(bias_ps)
+
+        grouped = sbuf.tile([P, PASSES, 4 * P], BF16, align_bytes=64)
+        codes = sbuf.tile([P, PASSES, P], U32, align_bytes=64)
+        act_planes = sbuf.tile([P, PASSES, P], U8, align_bytes=64)
+
+        def regroup(g):
+            nc.vector.tensor_copy(
+                out=grouped[:, g, :].bitcast(F32).rearrange("p (b u) -> p b u", u=2),
+                in_=flipped[g][:].rearrange("p u b -> p b u"),
+            )
+
+        def quantise(g):
+            nc.vector.quantize_mx(out=codes[:, g, :].bitcast(FP8X4), scales=act_planes[:, g, :], in_=grouped[:, g, :])
+
+        regroup(0)
+        regroup(1)
+        quantise(0)
+        regroup(2)
+        quantise(1)
+        quantise(2)
+        for k in range(BANKS):
+            nc.vector.tensor_copy(out=bias_sb[:, halves[k]], in_=bias_banks[k][:])
+        ratio = sbuf.tile([P, D_H], F32)
+        for cols in halves:
+            nc.vector.tensor_tensor(out=ratio[:, cols], in0=c_sb[:, cols], in1=half_recip[:, cols], op=ALU.mult)
+
+        acc = [psum.tile([P, BANK], F32, name="acc%d" % k) for k in range(BANKS)]
+        for g in range(PASSES):
+            for k in range(BANKS):
+                nc.tensor.matmul_mx(
+                    out=acc[k][:],
+                    lhsT=codes[:, g, :].bitcast(FP8X4),
+                    lhsT_scale=act_planes[:, g, :],
+                    rhs=words[:, g, 2 * k * BANK : 2 * (k + 1) * BANK].bitcast(FP4X4),
+                    rhs_scale=planes[:, g, halves[k]],
+                    start=(g == 0),
+                    stop=(g == PASSES - 1),
+                )
+
+        z = sbuf.tile([P, D_H], F32)
+        th = sbuf.tile([P, D_H], F32)
+        h_new = sbuf.tile([P, D_H], F32)
+        for k in range(BANKS):
+            nc.vector.tensor_tensor(out=z[:, halves[k]], in0=acc[k][:], in1=bias_sb[:, halves[k]], op=ALU.add)
+            nc.scalar.activation(out=th[:, halves[k]], in_=z[:, halves[k]], func=ACT.Tanh, scale=0.5)
+        for cols in halves:
+            nc.vector.scalar_tensor_tensor(
+                out=h_new[:, cols], in0=th[:, cols], scalar=1.0, in1=ratio[:, cols], op0=ALU.add, op1=ALU.mult
+            )
+            nc.sync.dma_start(out=out[:, cols], in_=h_new[:, cols])

@@ -45,21 +45,24 @@ def tile_slstmcell_pb_s_kernel(
 
         bias_rows = sbuf.tile([P, D_H], BF16)
         nc.vector.memset(bias_rows[:].bitcast(I32), 0)
+        nc.scalar.dma_start(out=bias_rows[0:1, :], in_=b_o.rearrange("(o n) -> o n", o=1))
+        two_eps = sbuf.tile([P, 1], F32)
+        nc.vector.memset(two_eps[:], 2.0 * EPS)
+        table_warmer = sbuf.tile([P, 1], F32)
+        nc.scalar.activation(out=table_warmer[:], in_=two_eps[:], func=ACT.Ln)
         planes = sbuf.tile([P, PASSES, D_H], U8, align_bytes=64)
         nc.vector.memset(planes[:].bitcast(I32), 0)
         ones = sbuf.tile([P, P], BF16)
         nc.vector.memset(ones[:], 1.0)
-        two_eps = sbuf.tile([P, 1], F32)
-        nc.vector.memset(two_eps[:], 2.0 * EPS)
         ident = sbuf.tile([P, P], F32)
         make_identity(nc, ident[:])
 
-        nc.scalar.dma_start(out=bias_rows[0:1, :], in_=b_o.rearrange("(o n) -> o n", o=1))
-        n_sb = sbuf.tile([P, D_H], BF16)
-        nc.sync.dma_start(out=n_sb[:], in_=n)
+
         acts = sbuf.tile([P, PASSES, K_PASS], BF16)
         nc.sync.dma_start(out=acts[:, 0, :], in_=x)
         nc.sync.dma_start(out=acts[:, 1:3, :], in_=h_prev.rearrange("b (g k) -> b g k", g=2))
+        n_sb = sbuf.tile([P, D_H], BF16)
+        nc.sync.dma_start(out=n_sb[:], in_=n)
         words = sbuf.tile([P, PASSES, 2 * D_H], U8, align_bytes=64)
         load_scale_rows(nc, planes[:, 0:1, :], W_o_scales)
         nc.sync.dma_start(out=words[:, 0, :].bitcast(I32), in_=W_o_words[0].bitcast(I32))
@@ -84,12 +87,9 @@ def tile_slstmcell_pb_s_kernel(
                 nc.tensor.transpose(flipped_g[:, u, :], pair_words[:, u : K_PASS // 2 : 2], ident[:])
             flipped.append(flipped_g)
 
-        bias_sb = sbuf.tile([P, D_H], F32)
-        bias_banks = []
-        for k in range(BANKS):
-            bias_ps = psum.tile([P, BANK], F32, name="bias_ps%d" % k)
-            nc.tensor.matmul(out=bias_ps[:], lhsT=ones[:], rhs=bias_rows[:, halves[k]], start=True, stop=True)
-            bias_banks.append(bias_ps)
+        bias_ps = psum.tile([P, D_H], BF16)
+        for cols in halves:
+            nc.tensor.matmul(out=bias_ps[:, cols], lhsT=ones[:], rhs=bias_rows[:, cols], start=True, stop=True)
 
         grouped = sbuf.tile([P, PASSES, 4 * P], BF16, align_bytes=64)
         codes = sbuf.tile([P, PASSES, P], U32, align_bytes=64)
@@ -110,11 +110,11 @@ def tile_slstmcell_pb_s_kernel(
         regroup(2)
         quantise(1)
         quantise(2)
-        for k in range(BANKS):
-            nc.vector.tensor_copy(out=bias_sb[:, halves[k]], in_=bias_banks[k][:])
+        bias_sb = sbuf.tile([P, D_H], BF16)
+        nc.vector.tensor_copy(out=bias_sb[:], in_=bias_ps[:])
         ratio = sbuf.tile([P, D_H], F32)
         for cols in halves:
-            nc.vector.tensor_tensor(out=ratio[:, cols], in0=c_sb[:, cols], in1=half_recip[:, cols], op=ALU.mult)
+            nc.gpsimd.tensor_tensor(out=ratio[:, cols], in0=c_sb[:, cols], in1=half_recip[:, cols], op=ALU.mult)
 
         acc = [psum.tile([P, BANK], F32, name="acc%d" % k) for k in range(BANKS)]
         for g in range(PASSES):

@@ -42,42 +42,45 @@ def tile_slstmcell_pb_s_kernel(
         psum = stack.enter_context(tc.psum_pool(name="psum", bufs=1))
         stack.enter_context(tc.manual_schedule())
         halves = [slice(k * BANK, (k + 1) * BANK) for k in range(BANKS)]
+        quarters = [slice(q * BANK // 2, (q + 1) * BANK // 2) for q in range(2 * BANKS)]
 
+        planes = sbuf.tile([P, PASSES, D_H], U8, align_bytes=64)
+        nc.vector.memset(planes[:].bitcast(I32), 0)
         bias_rows = sbuf.tile([P, D_H], BF16)
         nc.vector.memset(bias_rows[:].bitcast(I32), 0)
-        nc.scalar.dma_start(out=bias_rows[0:1, :], in_=b_o.rearrange("(o n) -> o n", o=1))
         two_eps = sbuf.tile([P, 1], F32)
         nc.vector.memset(two_eps[:], 2.0 * EPS)
         table_warmer = sbuf.tile([P, 1], F32)
         nc.scalar.activation(out=table_warmer[:], in_=two_eps[:], func=ACT.Ln)
-        planes = sbuf.tile([P, PASSES, D_H], U8, align_bytes=64)
-        nc.vector.memset(planes[:].bitcast(I32), 0)
         ones = sbuf.tile([P, P], BF16)
         nc.vector.memset(ones[:], 1.0)
         ident = sbuf.tile([P, P], F32)
         make_identity(nc, ident[:])
 
 
+        nc.gpsimd.dma_start(out=bias_rows[0:1, :], in_=b_o.rearrange("(o n) -> o n", o=1))
         acts = sbuf.tile([P, PASSES, K_PASS], BF16)
+        words = sbuf.tile([P, PASSES, 2 * D_H], U8, align_bytes=64)
+        n_sb = sbuf.tile([P, D_H], BF16)
+        c_sb = sbuf.tile([P, D_H], BF16)
         nc.sync.dma_start(out=acts[:, 0, :], in_=x)
         nc.sync.dma_start(out=acts[:, 1:3, :], in_=h_prev.rearrange("b (g k) -> b g k", g=2))
-        n_sb = sbuf.tile([P, D_H], BF16)
         nc.sync.dma_start(out=n_sb[:], in_=n)
-        words = sbuf.tile([P, PASSES, 2 * D_H], U8, align_bytes=64)
         load_scale_rows(nc, planes[:, 0:1, :], W_o_scales)
         nc.sync.dma_start(out=words[:, 0, :].bitcast(I32), in_=W_o_words[0].bitcast(I32))
         nc.sync.dma_start(out=words[:, 1, :].bitcast(I32), in_=U_o_words[0].bitcast(I32))
         load_scale_rows(nc, planes[:, 1:3, :], U_o_scales)
         nc.sync.dma_start(out=words[:, 2, :].bitcast(I32), in_=U_o_words[1].bitcast(I32))
-        c_sb = sbuf.tile([P, D_H], BF16)
         nc.sync.dma_start(out=c_sb[:], in_=c)
 
         log_2n = sbuf.tile([P, D_H], F32)
         half_recip = sbuf.tile([P, D_H], F32)
         for cols in halves:
             nc.scalar.activation(out=log_2n[:, cols], in_=n_sb[:, cols], func=ACT.Ln, bias=two_eps[:, 0:1], scale=2.0)
-        for cols in halves:
+        ratio = sbuf.tile([P, D_H], F32)
+        for cols in quarters:
             nc.scalar.activation(out=half_recip[:, cols], in_=log_2n[:, cols], func=ACT.Exp, scale=-1.0)
+            nc.gpsimd.tensor_tensor(out=ratio[:, cols], in0=c_sb[:, cols], in1=half_recip[:, cols], op=ALU.mult)
 
         flipped = []
         for g in range(PASSES):
@@ -86,10 +89,6 @@ def tile_slstmcell_pb_s_kernel(
             for u in range(2):
                 nc.tensor.transpose(flipped_g[:, u, :], pair_words[:, u : K_PASS // 2 : 2], ident[:])
             flipped.append(flipped_g)
-
-        bias_ps = psum.tile([P, D_H], BF16)
-        for cols in halves:
-            nc.tensor.matmul(out=bias_ps[:, cols], lhsT=ones[:], rhs=bias_rows[:, cols], start=True, stop=True)
 
         grouped = sbuf.tile([P, PASSES, 4 * P], BF16, align_bytes=64)
         codes = sbuf.tile([P, PASSES, P], U32, align_bytes=64)
@@ -110,12 +109,8 @@ def tile_slstmcell_pb_s_kernel(
         regroup(2)
         quantise(1)
         quantise(2)
-        bias_sb = sbuf.tile([P, D_H], BF16)
-        nc.vector.tensor_copy(out=bias_sb[:], in_=bias_ps[:])
-        ratio = sbuf.tile([P, D_H], F32)
-        for cols in halves:
-            nc.gpsimd.tensor_tensor(out=ratio[:, cols], in0=c_sb[:, cols], in1=half_recip[:, cols], op=ALU.mult)
 
+        bias_ps = psum.tile([P, D_H], BF16)
         acc = [psum.tile([P, BANK], F32, name="acc%d" % k) for k in range(BANKS)]
         for g in range(PASSES):
             for k in range(BANKS):
@@ -128,7 +123,12 @@ def tile_slstmcell_pb_s_kernel(
                     start=(g == 0),
                     stop=(g == PASSES - 1),
                 )
+            if g == 0:
+                for cols in halves:
+                    nc.tensor.matmul(out=bias_ps[:, cols], lhsT=ones[:], rhs=bias_rows[:, cols], start=True, stop=True)
 
+        bias_sb = sbuf.tile([P, D_H], BF16)
+        nc.vector.tensor_copy(out=bias_sb[:], in_=bias_ps[:])
         z = sbuf.tile([P, D_H], F32)
         th = sbuf.tile([P, D_H], F32)
         h_new = sbuf.tile([P, D_H], F32)

@@ -42,45 +42,45 @@ def tile_slstmcell_pb_s_kernel(
         psum = stack.enter_context(tc.psum_pool(name="psum", bufs=1))
         stack.enter_context(tc.manual_schedule())
         halves = [slice(k * BANK, (k + 1) * BANK) for k in range(BANKS)]
-        quarters = [slice(q * BANK // 2, (q + 1) * BANK // 2) for q in range(2 * BANKS)]
 
-        planes = sbuf.tile([P, PASSES, D_H], U8, align_bytes=64)
-        nc.vector.memset(planes[:].bitcast(I32), 0)
         bias_rows = sbuf.tile([P, D_H], BF16)
         nc.vector.memset(bias_rows[:].bitcast(I32), 0)
+        nc.scalar.dma_start(out=bias_rows[0:1, :], in_=b_o.rearrange("(o n) -> o n", o=1))
         two_eps = sbuf.tile([P, 1], F32)
         nc.vector.memset(two_eps[:], 2.0 * EPS)
         table_warmer = sbuf.tile([P, 1], F32)
         nc.scalar.activation(out=table_warmer[:], in_=two_eps[:], func=ACT.Ln)
+        w_planes = sbuf.tile([P, 1, D_H], U8, align_bytes=64)
+        nc.vector.memset(w_planes[:].bitcast(I32), 0)
+        u_planes = sbuf.tile([P, 2, D_H], U8, align_bytes=64)
+        nc.vector.memset(u_planes[:].bitcast(I32), 0)
+        planes = [w_planes[:, 0, :], u_planes[:, 0, :], u_planes[:, 1, :]]
         ones = sbuf.tile([P, P], BF16)
         nc.vector.memset(ones[:], 1.0)
         ident = sbuf.tile([P, P], F32)
         make_identity(nc, ident[:])
 
 
-        nc.gpsimd.dma_start(out=bias_rows[0:1, :], in_=b_o.rearrange("(o n) -> o n", o=1))
         acts = sbuf.tile([P, PASSES, K_PASS], BF16)
-        words = sbuf.tile([P, PASSES, 2 * D_H], U8, align_bytes=64)
-        n_sb = sbuf.tile([P, D_H], BF16)
-        c_sb = sbuf.tile([P, D_H], BF16)
         nc.sync.dma_start(out=acts[:, 0, :], in_=x)
         nc.sync.dma_start(out=acts[:, 1:3, :], in_=h_prev.rearrange("b (g k) -> b g k", g=2))
+        n_sb = sbuf.tile([P, D_H], BF16)
         nc.sync.dma_start(out=n_sb[:], in_=n)
-        load_scale_rows(nc, planes[:, 0:1, :], W_o_scales)
-        nc.sync.dma_start(out=words[:, 0, :].bitcast(I32), in_=W_o_words[0].bitcast(I32))
-        nc.sync.dma_start(out=words[:, 1, :].bitcast(I32), in_=U_o_words[0].bitcast(I32))
-        load_scale_rows(nc, planes[:, 1:3, :], U_o_scales)
-        nc.sync.dma_start(out=words[:, 2, :].bitcast(I32), in_=U_o_words[1].bitcast(I32))
+        words = [sbuf.tile([P, 2 * D_H], U8, align_bytes=64, name="words%d" % g) for g in range(PASSES)]
+        load_scale_rows(nc, w_planes, W_o_scales)
+        nc.sync.dma_start(out=words[0][:].bitcast(I32), in_=W_o_words[0].bitcast(I32))
+        nc.sync.dma_start(out=words[1][:].bitcast(I32), in_=U_o_words[0].bitcast(I32))
+        load_scale_rows(nc, u_planes, U_o_scales)
+        nc.sync.dma_start(out=words[2][:].bitcast(I32), in_=U_o_words[1].bitcast(I32))
+        c_sb = sbuf.tile([P, D_H], BF16)
         nc.sync.dma_start(out=c_sb[:], in_=c)
 
         log_2n = sbuf.tile([P, D_H], F32)
         half_recip = sbuf.tile([P, D_H], F32)
         for cols in halves:
             nc.scalar.activation(out=log_2n[:, cols], in_=n_sb[:, cols], func=ACT.Ln, bias=two_eps[:, 0:1], scale=2.0)
-        ratio = sbuf.tile([P, D_H], F32)
-        for cols in quarters:
+        for cols in halves:
             nc.scalar.activation(out=half_recip[:, cols], in_=log_2n[:, cols], func=ACT.Exp, scale=-1.0)
-            nc.gpsimd.tensor_tensor(out=ratio[:, cols], in0=c_sb[:, cols], in1=half_recip[:, cols], op=ALU.mult)
 
         flipped = []
         for g in range(PASSES):
@@ -90,18 +90,22 @@ def tile_slstmcell_pb_s_kernel(
                 nc.tensor.transpose(flipped_g[:, u, :], pair_words[:, u : K_PASS // 2 : 2], ident[:])
             flipped.append(flipped_g)
 
-        grouped = sbuf.tile([P, PASSES, 4 * P], BF16, align_bytes=64)
-        codes = sbuf.tile([P, PASSES, P], U32, align_bytes=64)
-        act_planes = sbuf.tile([P, PASSES, P], U8, align_bytes=64)
+        bias_ps = psum.tile([P, D_H], BF16)
+        for cols in halves:
+            nc.tensor.matmul(out=bias_ps[:, cols], lhsT=ones[:], rhs=bias_rows[:, cols], start=True, stop=True)
+
+        grouped = [sbuf.tile([P, 4 * P], BF16, align_bytes=64, name="grouped%d" % g) for g in range(PASSES)]
+        codes = [sbuf.tile([P, P], U32, align_bytes=64, name="codes%d" % g) for g in range(PASSES)]
+        act_planes = [sbuf.tile([P, P], U8, align_bytes=64, name="act_plane%d" % g) for g in range(PASSES)]
 
         def regroup(g):
             nc.vector.tensor_copy(
-                out=grouped[:, g, :].bitcast(F32).rearrange("p (b u) -> p b u", u=2),
+                out=grouped[g][:].bitcast(F32).rearrange("p (b u) -> p b u", u=2),
                 in_=flipped[g][:].rearrange("p u b -> p b u"),
             )
 
         def quantise(g):
-            nc.vector.quantize_mx(out=codes[:, g, :].bitcast(FP8X4), scales=act_planes[:, g, :], in_=grouped[:, g, :])
+            nc.vector.quantize_mx(out=codes[g][:].bitcast(FP8X4), scales=act_planes[g][:], in_=grouped[g][:])
 
         regroup(0)
         regroup(1)
@@ -109,26 +113,25 @@ def tile_slstmcell_pb_s_kernel(
         regroup(2)
         quantise(1)
         quantise(2)
+        bias_sb = sbuf.tile([P, D_H], BF16)
+        nc.vector.tensor_copy(out=bias_sb[:], in_=bias_ps[:])
+        ratio = sbuf.tile([P, D_H], F32)
+        for cols in halves:
+            nc.gpsimd.tensor_tensor(out=ratio[:, cols], in0=c_sb[:, cols], in1=half_recip[:, cols], op=ALU.mult)
 
-        bias_ps = psum.tile([P, D_H], BF16)
         acc = [psum.tile([P, BANK], F32, name="acc%d" % k) for k in range(BANKS)]
         for g in range(PASSES):
             for k in range(BANKS):
                 nc.tensor.matmul_mx(
                     out=acc[k][:],
-                    lhsT=codes[:, g, :].bitcast(FP8X4),
-                    lhsT_scale=act_planes[:, g, :],
-                    rhs=words[:, g, 2 * k * BANK : 2 * (k + 1) * BANK].bitcast(FP4X4),
-                    rhs_scale=planes[:, g, halves[k]],
+                    lhsT=codes[g][:].bitcast(FP8X4),
+                    lhsT_scale=act_planes[g][:],
+                    rhs=words[g][:, 2 * k * BANK : 2 * (k + 1) * BANK].bitcast(FP4X4),
+                    rhs_scale=planes[g][:, halves[k]],
                     start=(g == 0),
                     stop=(g == PASSES - 1),
                 )
-            if g == 0:
-                for cols in halves:
-                    nc.tensor.matmul(out=bias_ps[:, cols], lhsT=ones[:], rhs=bias_rows[:, cols], start=True, stop=True)
 
-        bias_sb = sbuf.tile([P, D_H], BF16)
-        nc.vector.tensor_copy(out=bias_sb[:], in_=bias_ps[:])
         z = sbuf.tile([P, D_H], F32)
         th = sbuf.tile([P, D_H], F32)
         h_new = sbuf.tile([P, D_H], F32)

@@ -18,8 +18,9 @@ D_IN = 512
 D_H = 1024
 K_PASS = 512
 PASSES = (D_IN + D_H) // K_PASS
-BANK = 512
-BANKS = D_H // BANK
+BLOCKS = D_H // P
+HALF = D_H // 2
+PAIRS = BLOCKS // 2
 EPS = 1e-6
 
 FLOPS = 2 * P * (D_IN + D_H) * D_H
@@ -41,58 +42,62 @@ def tile_slstmcell_pb_s_kernel(
         sbuf = stack.enter_context(tc.tile_pool(name="sbuf", bufs=1))
         psum = stack.enter_context(tc.psum_pool(name="psum", bufs=1))
         stack.enter_context(tc.manual_schedule())
-        halves = [slice(k * BANK, (k + 1) * BANK) for k in range(BANKS)]
+        halves = [slice(k * HALF, (k + 1) * HALF) for k in range(2)]
 
-        bias_rows = sbuf.tile([P, D_H], BF16)
-        nc.vector.memset(bias_rows[:].bitcast(I32), 0)
-        nc.scalar.dma_start(out=bias_rows[0:1, :], in_=b_o.rearrange("(o n) -> o n", o=1))
+        bias_rows = sbuf.tile([P, P], BF16)
+        nc.vector.memset(bias_rows[:], 0.0)
+        nc.scalar.dma_start(out=bias_rows[0:BLOCKS, :], in_=b_o.rearrange("(j p) -> j p", p=P))
         two_eps = sbuf.tile([P, 1], F32)
         nc.vector.memset(two_eps[:], 2.0 * EPS)
         table_warmer = sbuf.tile([P, 1], F32)
-        nc.scalar.activation(out=table_warmer[:], in_=two_eps[:], func=ACT.Ln)
+        nc.scalar.activation(out=table_warmer[:], in_=two_eps[:], func=ACT.Abs_reciprocal_sqrt)
         w_planes = sbuf.tile([P, 1, D_H], U8, align_bytes=64)
         nc.vector.memset(w_planes[:].bitcast(I32), 0)
         u_planes = sbuf.tile([P, 2, D_H], U8, align_bytes=64)
         nc.vector.memset(u_planes[:].bitcast(I32), 0)
         planes = [w_planes[:, 0, :], u_planes[:, 0, :], u_planes[:, 1, :]]
-        ones = sbuf.tile([P, P], BF16)
-        nc.vector.memset(ones[:], 1.0)
+
+        c_sb = sbuf.tile([P, D_H], BF16)
+        nc.gpsimd.dma_start(out=c_sb[:], in_=c)
         ident = sbuf.tile([P, P], F32)
         make_identity(nc, ident[:])
-
 
         acts = sbuf.tile([P, PASSES, K_PASS], BF16)
         nc.sync.dma_start(out=acts[:, 0, :], in_=x)
         nc.sync.dma_start(out=acts[:, 1:3, :], in_=h_prev.rearrange("b (g k) -> b g k", g=2))
         n_sb = sbuf.tile([P, D_H], BF16)
         nc.sync.dma_start(out=n_sb[:], in_=n)
-        words = [sbuf.tile([P, 2 * D_H], U8, align_bytes=64, name="words%d" % g) for g in range(PASSES)]
         load_scale_rows(nc, w_planes, W_o_scales)
-        nc.sync.dma_start(out=words[0][:].bitcast(I32), in_=W_o_words[0].bitcast(I32))
-        nc.sync.dma_start(out=words[1][:].bitcast(I32), in_=U_o_words[0].bitcast(I32))
+        w_words = sbuf.tile([P, 2 * D_H], U8, align_bytes=64)
+        nc.sync.dma_start(out=w_words[:].bitcast(I32), in_=W_o_words[0].bitcast(I32))
+        u_words = [sbuf.tile([P, 2, 2 * HALF], U8, align_bytes=64, name="u_words%d" % k) for k in range(2)]
+        for k in range(2):
+            nc.sync.dma_start(
+                out=u_words[k][:].bitcast(I32),
+                in_=U_o_words[:, :, 2 * HALF * k : 2 * HALF * (k + 1)].rearrange("g p w -> p g w").bitcast(I32),
+            )
         load_scale_rows(nc, u_planes, U_o_scales)
-        nc.sync.dma_start(out=words[2][:].bitcast(I32), in_=U_o_words[1].bitcast(I32))
-        c_sb = sbuf.tile([P, D_H], BF16)
-        nc.sync.dma_start(out=c_sb[:], in_=c)
 
-        log_2n = sbuf.tile([P, D_H], F32)
-        half_recip = sbuf.tile([P, D_H], F32)
+        root = sbuf.tile([P, D_H], F32)
         for cols in halves:
-            nc.scalar.activation(out=log_2n[:, cols], in_=n_sb[:, cols], func=ACT.Ln, bias=two_eps[:, 0:1], scale=2.0)
-        for cols in halves:
-            nc.scalar.activation(out=half_recip[:, cols], in_=log_2n[:, cols], func=ACT.Exp, scale=-1.0)
+            nc.scalar.activation(
+                out=root[:, cols], in_=n_sb[:, cols], func=ACT.Abs_reciprocal_sqrt, bias=two_eps[:, 0:1], scale=2.0
+            )
+        tanh_warmer = sbuf.tile([P, 1], F32)
+        nc.scalar.activation(out=tanh_warmer[:], in_=two_eps[:], func=ACT.Tanh)
 
         flipped = []
         for g in range(PASSES):
             pair_words = acts[:, g, :].bitcast(F32)
-            flipped_g = psum.tile([P, 2, P], F32, name="flipped%d" % g)
+            flipped_g = psum.tile([P, 2, P], F32, name="flipped%d" % g, tag="bank%d" % g)
             for u in range(2):
                 nc.tensor.transpose(flipped_g[:, u, :], pair_words[:, u : K_PASS // 2 : 2], ident[:])
             flipped.append(flipped_g)
 
-        bias_ps = psum.tile([P, D_H], BF16)
-        for cols in halves:
-            nc.tensor.matmul(out=bias_ps[:, cols], lhsT=ones[:], rhs=bias_rows[:, cols], start=True, stop=True)
+        ident_bf = sbuf.tile([P, P], BF16)
+        nc.vector.tensor_copy(out=ident_bf[:], in_=ident[:])
+        bias_ps = psum.tile([P, P], BF16, tag="bank3")
+        nc.tensor.transpose(bias_ps[:], bias_rows[:], ident_bf[:])
 
         grouped = [sbuf.tile([P, 4 * P], BF16, align_bytes=64, name="grouped%d" % g) for g in range(PASSES)]
         codes = [sbuf.tile([P, P], U32, align_bytes=64, name="codes%d" % g) for g in range(PASSES)]
@@ -113,33 +118,55 @@ def tile_slstmcell_pb_s_kernel(
         regroup(2)
         quantise(1)
         quantise(2)
-        bias_sb = sbuf.tile([P, D_H], BF16)
-        nc.vector.tensor_copy(out=bias_sb[:], in_=bias_ps[:])
+        half_bias = sbuf.tile([P, BLOCKS], F32)
+        nc.vector.tensor_scalar(out=half_bias[:], in0=bias_ps[:, 0:BLOCKS], scalar1=0.5, scalar2=None, op0=ALU.mult)
+        c_root = sbuf.tile([P, D_H], F32)
         ratio = sbuf.tile([P, D_H], F32)
         for cols in halves:
-            nc.gpsimd.tensor_tensor(out=ratio[:, cols], in0=c_sb[:, cols], in1=half_recip[:, cols], op=ALU.mult)
-
-        acc = [psum.tile([P, BANK], F32, name="acc%d" % k) for k in range(BANKS)]
-        for g in range(PASSES):
-            for k in range(BANKS):
-                nc.tensor.matmul_mx(
-                    out=acc[k][:],
-                    lhsT=codes[g][:].bitcast(FP8X4),
-                    lhsT_scale=act_planes[g][:],
-                    rhs=words[g][:, 2 * k * BANK : 2 * (k + 1) * BANK].bitcast(FP4X4),
-                    rhs_scale=planes[g][:, halves[k]],
-                    start=(g == 0),
-                    stop=(g == PASSES - 1),
-                )
-
-        z = sbuf.tile([P, D_H], F32)
-        th = sbuf.tile([P, D_H], F32)
-        h_new = sbuf.tile([P, D_H], F32)
-        for k in range(BANKS):
-            nc.vector.tensor_tensor(out=z[:, halves[k]], in0=acc[k][:], in1=bias_sb[:, halves[k]], op=ALU.add)
-            nc.scalar.activation(out=th[:, halves[k]], in_=z[:, halves[k]], func=ACT.Tanh, scale=0.5)
+            nc.gpsimd.tensor_tensor(out=c_root[:, cols], in0=c_sb[:, cols], in1=root[:, cols], op=ALU.mult)
         for cols in halves:
+            nc.vector.tensor_tensor(out=ratio[:, cols], in0=c_root[:, cols], in1=root[:, cols], op=ALU.mult)
+
+        acc = [psum.tile([P, P], F32, name="acc%d" % j, tag="bank%d" % j) for j in range(BLOCKS)]
+        th = [sbuf.tile([P, 2, P], F32, name="th%d" % i) for i in range(PAIRS)]
+
+        def multiply(j, g):
+            if g == 0:
+                words = w_words[:, 2 * P * j : 2 * P * (j + 1)]
+            else:
+                k, i = divmod(j, BLOCKS // 2)
+                words = u_words[k][:, g - 1, 2 * P * i : 2 * P * (i + 1)]
+            nc.tensor.matmul_mx(
+                out=acc[j][:],
+                lhsT=words.bitcast(FP4X4),
+                lhsT_scale=planes[g][:, P * j : P * (j + 1)],
+                rhs=codes[g][:].bitcast(FP8X4),
+                rhs_scale=act_planes[g][:],
+                start=(g == 0),
+                stop=(g == PASSES - 1),
+            )
+
+        for j in range(BLOCKS):
+            multiply(j, 0)
+        for j in range(BLOCKS):
+            multiply(j, 1)
+            multiply(j, 2)
+            nc.scalar.activation(
+                out=th[j // 2][:, j % 2, :], in_=acc[j][:], func=ACT.Tanh, bias=half_bias[:, j : j + 1], scale=0.5
+            )
+
+        h_new = sbuf.tile([P, D_H], F32)
+        for i in range(PAIRS):
+            cols = slice(2 * P * i, 2 * P * (i + 1))
+            th_rows = psum.tile([P, 2, P], F32, name="th_rows%d" % i, tag="bank%d" % i)
+            for j in range(2):
+                nc.tensor.transpose(th_rows[:, j, :], th[i][:, j, :], ident[:])
             nc.vector.scalar_tensor_tensor(
-                out=h_new[:, cols], in0=th[:, cols], scalar=1.0, in1=ratio[:, cols], op0=ALU.add, op1=ALU.mult
+                out=h_new[:, cols],
+                in0=th_rows[:].rearrange("p j b -> p (j b)"),
+                scalar=1.0,
+                in1=ratio[:, cols],
+                op0=ALU.add,
+                op1=ALU.mult,
             )
             nc.sync.dma_start(out=out[:, cols], in_=h_new[:, cols])

@@ -21,6 +21,7 @@ PASSES = (D_IN + D_H) // K_PASS
 BLOCKS = D_H // P
 HALF = D_H // 2
 PAIRS = BLOCKS // 2
+ORDER = (1, 2, 0)
 EPS = 1e-6
 
 FLOPS = 2 * P * (D_IN + D_H) * D_H
@@ -47,14 +48,16 @@ def tile_slstmcell_pb_s_kernel(
         bias_rows = sbuf.tile([P, P], BF16)
         nc.vector.memset(bias_rows[:], 0.0)
         nc.scalar.dma_start(out=bias_rows[0:BLOCKS, :], in_=b_o.rearrange("(j p) -> j p", p=P))
+        idle_in = sbuf.tile([P, 2 * P], F32)
+        nc.vector.memset(idle_in[:], 1.0)
         two_eps = sbuf.tile([P, 1], F32)
         nc.vector.memset(two_eps[:], 2.0 * EPS)
         table_warmer = sbuf.tile([P, 1], F32)
         nc.scalar.activation(out=table_warmer[:], in_=two_eps[:], func=ACT.Abs_reciprocal_sqrt)
-        w_planes = sbuf.tile([P, 1, D_H], U8, align_bytes=64)
-        nc.vector.memset(w_planes[:].bitcast(I32), 0)
         u_planes = sbuf.tile([P, 2, D_H], U8, align_bytes=64)
         nc.vector.memset(u_planes[:].bitcast(I32), 0)
+        w_planes = sbuf.tile([P, 1, D_H], U8, align_bytes=64)
+        nc.vector.memset(w_planes[:].bitcast(I32), 0)
         planes = [w_planes[:, 0, :], u_planes[:, 0, :], u_planes[:, 1, :]]
 
         c_sb = sbuf.tile([P, D_H], BF16)
@@ -63,20 +66,24 @@ def tile_slstmcell_pb_s_kernel(
         make_identity(nc, ident[:])
 
         acts = sbuf.tile([P, PASSES, K_PASS], BF16)
-        nc.sync.dma_start(out=acts[:, 0, :], in_=x)
         nc.sync.dma_start(out=acts[:, 1:3, :], in_=h_prev.rearrange("b (g k) -> b g k", g=2))
         n_sb = sbuf.tile([P, D_H], BF16)
         nc.sync.dma_start(out=n_sb[:], in_=n)
-        load_scale_rows(nc, w_planes, W_o_scales)
-        w_words = sbuf.tile([P, 2 * D_H], U8, align_bytes=64)
-        nc.sync.dma_start(out=w_words[:].bitcast(I32), in_=W_o_words[0].bitcast(I32))
+        nc.sync.dma_start(out=acts[:, 0, :], in_=x)
+        load_scale_rows(nc, u_planes, U_o_scales)
         u_words = [sbuf.tile([P, 2, 2 * HALF], U8, align_bytes=64, name="u_words%d" % k) for k in range(2)]
-        for k in range(2):
+
+        def load_u(k):
             nc.sync.dma_start(
                 out=u_words[k][:].bitcast(I32),
                 in_=U_o_words[:, :, 2 * HALF * k : 2 * HALF * (k + 1)].rearrange("g p w -> p g w").bitcast(I32),
             )
-        load_scale_rows(nc, u_planes, U_o_scales)
+
+        load_u(0)
+        w_words = sbuf.tile([P, 2 * D_H], U8, align_bytes=64)
+        nc.sync.dma_start(out=w_words[:].bitcast(I32), in_=W_o_words[0].bitcast(I32))
+        load_scale_rows(nc, w_planes, W_o_scales)
+        load_u(1)
 
         root = sbuf.tile([P, D_H], F32)
         for cols in halves:
@@ -86,18 +93,28 @@ def tile_slstmcell_pb_s_kernel(
         tanh_warmer = sbuf.tile([P, 1], F32)
         nc.scalar.activation(out=tanh_warmer[:], in_=two_eps[:], func=ACT.Tanh)
 
-        flipped = []
-        for g in range(PASSES):
+        idle_out = psum.tile([P, 2 * P], F32, tag="bank7")
+
+        def keep_warm():
+            nc.tensor.matmul(out=idle_out[:], lhsT=idle_in[:, 0:P], rhs=idle_in[:], start=True, stop=True)
+
+        keep_warm()
+        keep_warm()
+
+        flipped = {}
+        for g in ORDER:
             pair_words = acts[:, g, :].bitcast(F32)
             flipped_g = psum.tile([P, 2, P], F32, name="flipped%d" % g, tag="bank%d" % g)
             for u in range(2):
                 nc.tensor.transpose(flipped_g[:, u, :], pair_words[:, u : K_PASS // 2 : 2], ident[:])
-            flipped.append(flipped_g)
+            flipped[g] = flipped_g
 
         ident_bf = sbuf.tile([P, P], BF16)
         nc.vector.tensor_copy(out=ident_bf[:], in_=ident[:])
         bias_ps = psum.tile([P, P], BF16, tag="bank3")
         nc.tensor.transpose(bias_ps[:], bias_rows[:], ident_bf[:])
+
+        keep_warm()
 
         grouped = [sbuf.tile([P, 4 * P], BF16, align_bytes=64, name="grouped%d" % g) for g in range(PASSES)]
         codes = [sbuf.tile([P, P], U32, align_bytes=64, name="codes%d" % g) for g in range(PASSES)]
@@ -112,19 +129,18 @@ def tile_slstmcell_pb_s_kernel(
         def quantise(g):
             nc.vector.quantize_mx(out=codes[g][:].bitcast(FP8X4), scales=act_planes[g][:], in_=grouped[g][:])
 
-        regroup(0)
         regroup(1)
-        quantise(0)
         regroup(2)
         quantise(1)
         quantise(2)
+        regroup(0)
         half_bias = sbuf.tile([P, BLOCKS], F32)
         nc.vector.tensor_scalar(out=half_bias[:], in0=bias_ps[:, 0:BLOCKS], scalar1=0.5, scalar2=None, op0=ALU.mult)
+        quantise(0)
         c_root = sbuf.tile([P, D_H], F32)
         ratio = sbuf.tile([P, D_H], F32)
         for cols in halves:
-            nc.gpsimd.tensor_tensor(out=c_root[:, cols], in0=c_sb[:, cols], in1=root[:, cols], op=ALU.mult)
-        for cols in halves:
+            nc.vector.tensor_tensor(out=c_root[:, cols], in0=c_sb[:, cols], in1=root[:, cols], op=ALU.mult)
             nc.vector.tensor_tensor(out=ratio[:, cols], in0=c_root[:, cols], in1=root[:, cols], op=ALU.mult)
 
         acc = [psum.tile([P, P], F32, name="acc%d" % j, tag="bank%d" % j) for j in range(BLOCKS)]
@@ -142,21 +158,18 @@ def tile_slstmcell_pb_s_kernel(
                 lhsT_scale=planes[g][:, P * j : P * (j + 1)],
                 rhs=codes[g][:].bitcast(FP8X4),
                 rhs_scale=act_planes[g][:],
-                start=(g == 0),
-                stop=(g == PASSES - 1),
+                start=(g == ORDER[0]),
+                stop=(g == ORDER[-1]),
             )
 
-        for j in range(BLOCKS):
-            multiply(j, 0)
-        for j in range(BLOCKS):
-            multiply(j, 1)
-            multiply(j, 2)
+        def gate(j):
             nc.scalar.activation(
                 out=th[j // 2][:, j % 2, :], in_=acc[j][:], func=ACT.Tanh, bias=half_bias[:, j : j + 1], scale=0.5
             )
 
         h_new = sbuf.tile([P, D_H], F32)
-        for i in range(PAIRS):
+
+        def finish(i):
             cols = slice(2 * P * i, 2 * P * (i + 1))
             th_rows = psum.tile([P, 2, P], F32, name="th_rows%d" % i, tag="bank%d" % i)
             for j in range(2):
@@ -170,3 +183,19 @@ def tile_slstmcell_pb_s_kernel(
                 op1=ALU.mult,
             )
             nc.sync.dma_start(out=out[:, cols], in_=h_new[:, cols])
+
+        for j in range(4):
+            multiply(j, 1)
+            multiply(j, 2)
+        for j in range(4):
+            multiply(j, 0)
+            gate(j)
+        for j in range(4, 8):
+            multiply(j, 1)
+            multiply(j, 2)
+        finish(0)
+        for j in range(4, 8):
+            multiply(j, 0)
+            gate(j)
+        for i in (1, 2, 3):
+            finish(i)

@@ -47,7 +47,6 @@ def tile_slstmcell_pb_s_kernel(
 
         bias_rows = sbuf.tile([P, P], BF16)
         nc.vector.memset(bias_rows[:], 0.0)
-        nc.scalar.dma_start(out=bias_rows[0:BLOCKS, :], in_=b_o.rearrange("(j p) -> j p", p=P))
         idle_in = sbuf.tile([P, 2 * P], F32)
         nc.vector.memset(idle_in[:], 1.0)
         two_eps = sbuf.tile([P, 1], F32)
@@ -82,6 +81,7 @@ def tile_slstmcell_pb_s_kernel(
         load_u(0)
         w_words = sbuf.tile([P, 2 * D_H], U8, align_bytes=64)
         nc.sync.dma_start(out=w_words[:].bitcast(I32), in_=W_o_words[0].bitcast(I32))
+        nc.sync.dma_start(out=bias_rows[0:BLOCKS, :], in_=b_o.rearrange("(j p) -> j p", p=P))
         load_scale_rows(nc, w_planes, W_o_scales)
         load_u(1)
 
@@ -93,13 +93,13 @@ def tile_slstmcell_pb_s_kernel(
         tanh_warmer = sbuf.tile([P, 1], F32)
         nc.scalar.activation(out=tanh_warmer[:], in_=two_eps[:], func=ACT.Tanh)
 
-        idle_out = psum.tile([P, 2 * P], F32, tag="bank7")
+        idle_out = psum.tile([P, 2 * P], F32, tag="bank6")
 
-        def keep_warm():
-            nc.tensor.matmul(out=idle_out[:], lhsT=idle_in[:, 0:P], rhs=idle_in[:], start=True, stop=True)
+        def keep_warm(width):
+            nc.tensor.matmul(out=idle_out[:, 0:width], lhsT=idle_in[:, 0:P], rhs=idle_in[:, 0:width], start=True, stop=True)
 
-        keep_warm()
-        keep_warm()
+        keep_warm(2 * P)
+        keep_warm(P)
 
         flipped = {}
         for g in ORDER:
@@ -111,10 +111,8 @@ def tile_slstmcell_pb_s_kernel(
 
         ident_bf = sbuf.tile([P, P], BF16)
         nc.vector.tensor_copy(out=ident_bf[:], in_=ident[:])
-        bias_ps = psum.tile([P, P], BF16, tag="bank3")
-        nc.tensor.transpose(bias_ps[:], bias_rows[:], ident_bf[:])
 
-        keep_warm()
+        keep_warm(2 * P)
 
         grouped = [sbuf.tile([P, 4 * P], BF16, align_bytes=64, name="grouped%d" % g) for g in range(PASSES)]
         codes = [sbuf.tile([P, P], U32, align_bytes=64, name="codes%d" % g) for g in range(PASSES)]
@@ -134,16 +132,13 @@ def tile_slstmcell_pb_s_kernel(
         quantise(1)
         quantise(2)
         regroup(0)
-        half_bias = sbuf.tile([P, BLOCKS], F32)
-        nc.vector.tensor_scalar(out=half_bias[:], in0=bias_ps[:, 0:BLOCKS], scalar1=0.5, scalar2=None, op0=ALU.mult)
         quantise(0)
         c_root = sbuf.tile([P, D_H], F32)
         ratio = sbuf.tile([P, D_H], F32)
         for cols in halves:
             nc.vector.tensor_tensor(out=c_root[:, cols], in0=c_sb[:, cols], in1=root[:, cols], op=ALU.mult)
-            nc.vector.tensor_tensor(out=ratio[:, cols], in0=c_root[:, cols], in1=root[:, cols], op=ALU.mult)
 
-        acc = [psum.tile([P, P], F32, name="acc%d" % j, tag="bank%d" % j) for j in range(BLOCKS)]
+        acc = {j: psum.tile([P, P], F32, name="acc%d" % j, tag="bank%d" % j) for j in range(4)}
         th = [sbuf.tile([P, 2, P], F32, name="th%d" % i) for i in range(PAIRS)]
 
         def multiply(j, g):
@@ -187,15 +182,23 @@ def tile_slstmcell_pb_s_kernel(
         for j in range(4):
             multiply(j, 1)
             multiply(j, 2)
+
+        bias_ps = psum.tile([P, P], BF16, tag="bank7")
+        nc.tensor.transpose(bias_ps[:], bias_rows[:], ident_bf[:])
+        half_bias = sbuf.tile([P, BLOCKS], F32)
+        nc.vector.tensor_scalar(out=half_bias[:], in0=bias_ps[:, 0:BLOCKS], scalar1=0.5, scalar2=None, op0=ALU.mult)
+        for cols in halves:
+            nc.vector.tensor_tensor(out=ratio[:, cols], in0=c_root[:, cols], in1=root[:, cols], op=ALU.mult)
+
         for j in range(4):
             multiply(j, 0)
             gate(j)
         for j in range(4, 8):
+            acc[j] = psum.tile([P, P], F32, name="acc%d" % j, tag="bank%d" % j)
             multiply(j, 1)
             multiply(j, 2)
-        finish(0)
         for j in range(4, 8):
             multiply(j, 0)
             gate(j)
-        for i in (1, 2, 3):
+        for i in range(PAIRS):
             finish(i)

@@ -22,6 +22,7 @@ BLOCKS = D_H // P
 HALF = D_H // 2
 PAIRS = BLOCKS // 2
 ORDER = (1, 2, 0)
+HEAD = 6
 EPS = 1e-6
 
 FLOPS = 2 * P * (D_IN + D_H) * D_H
@@ -70,12 +71,14 @@ def tile_slstmcell_pb_s_kernel(
         nc.sync.dma_start(out=n_sb[:], in_=n)
         nc.sync.dma_start(out=acts[:, 0, :], in_=x)
         load_scale_rows(nc, u_planes, U_o_scales)
-        u_words = [sbuf.tile([P, 2, 2 * HALF], U8, align_bytes=64, name="u_words%d" % k) for k in range(2)]
+        cuts = ((0, HEAD), (HEAD, BLOCKS))
+        u_words = [sbuf.tile([P, 2, 2 * P * (b - a)], U8, align_bytes=64, name="u_words%d" % a) for a, b in cuts]
 
         def load_u(k):
+            a, b = cuts[k]
             nc.sync.dma_start(
                 out=u_words[k][:].bitcast(I32),
-                in_=U_o_words[:, :, 2 * HALF * k : 2 * HALF * (k + 1)].rearrange("g p w -> p g w").bitcast(I32),
+                in_=U_o_words[:, :, 2 * P * a : 2 * P * b].rearrange("g p w -> p g w").bitcast(I32),
             )
 
         load_u(0)
@@ -138,14 +141,15 @@ def tile_slstmcell_pb_s_kernel(
         for cols in halves:
             nc.vector.tensor_tensor(out=c_root[:, cols], in0=c_sb[:, cols], in1=root[:, cols], op=ALU.mult)
 
-        acc = {j: psum.tile([P, P], F32, name="acc%d" % j, tag="bank%d" % j) for j in range(4)}
+        acc = {j: psum.tile([P, P], F32, name="acc%d" % j, tag="bank%d" % j) for j in range(HEAD)}
         th = [sbuf.tile([P, 2, P], F32, name="th%d" % i) for i in range(PAIRS)]
 
         def multiply(j, g):
             if g == 0:
                 words = w_words[:, 2 * P * j : 2 * P * (j + 1)]
             else:
-                k, i = divmod(j, BLOCKS // 2)
+                k = int(j >= HEAD)
+                i = j - cuts[k][0]
                 words = u_words[k][:, g - 1, 2 * P * i : 2 * P * (i + 1)]
             nc.tensor.matmul_mx(
                 out=acc[j][:],
@@ -179,7 +183,7 @@ def tile_slstmcell_pb_s_kernel(
             )
             nc.sync.dma_start(out=out[:, cols], in_=h_new[:, cols])
 
-        for j in range(4):
+        for j in range(HEAD):
             multiply(j, 1)
             multiply(j, 2)
 
@@ -190,14 +194,14 @@ def tile_slstmcell_pb_s_kernel(
         for cols in halves:
             nc.vector.tensor_tensor(out=ratio[:, cols], in0=c_root[:, cols], in1=root[:, cols], op=ALU.mult)
 
-        for j in range(4):
+        for j in range(HEAD):
             multiply(j, 0)
             gate(j)
-        for j in range(4, 8):
+        for j in range(HEAD, BLOCKS):
             acc[j] = psum.tile([P, P], F32, name="acc%d" % j, tag="bank%d" % j)
             multiply(j, 1)
             multiply(j, 2)
-        for j in range(4, 8):
+        for j in range(HEAD, BLOCKS):
             multiply(j, 0)
             gate(j)
         for i in range(PAIRS):

@@ -82,9 +82,9 @@ def tile_slstmcell_pb_s_kernel(
             )
 
         load_u(0)
+        nc.sync.dma_start(out=bias_rows[0:BLOCKS, :], in_=b_o.rearrange("(j p) -> j p", p=P))
         w_words = sbuf.tile([P, 2 * D_H], U8, align_bytes=64)
         nc.sync.dma_start(out=w_words[:].bitcast(I32), in_=W_o_words[0].bitcast(I32))
-        nc.sync.dma_start(out=bias_rows[0:BLOCKS, :], in_=b_o.rearrange("(j p) -> j p", p=P))
         load_scale_rows(nc, w_planes, W_o_scales)
         load_u(1)
 
@@ -93,10 +93,8 @@ def tile_slstmcell_pb_s_kernel(
             nc.scalar.activation(
                 out=root[:, cols], in_=n_sb[:, cols], func=ACT.Abs_reciprocal_sqrt, bias=two_eps[:, 0:1], scale=2.0
             )
-        tanh_warmer = sbuf.tile([P, 1], F32)
-        nc.scalar.activation(out=tanh_warmer[:], in_=two_eps[:], func=ACT.Tanh)
 
-        idle_out = psum.tile([P, 2 * P], F32, tag="bank6")
+        idle_out = psum.tile([P, 2 * P], F32, tag="bank5")
 
         def keep_warm(width):
             nc.tensor.matmul(out=idle_out[:, 0:width], lhsT=idle_in[:, 0:P], rhs=idle_in[:, 0:width], start=True, stop=True)
@@ -104,19 +102,26 @@ def tile_slstmcell_pb_s_kernel(
         keep_warm(2 * P)
         keep_warm(P)
 
-        flipped = {}
-        for g in ORDER:
+        flipped = [psum.tile([P, 2, P], F32, name="flipped%d" % b, tag="bank%d" % b) for b in (7, 0, 1)]
+
+        def flip(g):
             pair_words = acts[:, g, :].bitcast(F32)
-            flipped_g = psum.tile([P, 2, P], F32, name="flipped%d" % g, tag="bank%d" % g)
             for u in range(2):
-                nc.tensor.transpose(flipped_g[:, u, :], pair_words[:, u : K_PASS // 2 : 2], ident[:])
-            flipped[g] = flipped_g
+                nc.tensor.transpose(flipped[g][:, u, :], pair_words[:, u : K_PASS // 2 : 2], ident[:])
+
+        flip(1)
+        flip(2)
+        flip(0)
+        keep_warm(2 * P)
 
         ident_bf = sbuf.tile([P, P], BF16)
         nc.vector.tensor_copy(out=ident_bf[:], in_=ident[:])
-
-        keep_warm(2 * P)
-
+        bias_ps = psum.tile([P, P], BF16, tag="bank6")
+        nc.tensor.transpose(bias_ps[:], bias_rows[:], ident_bf[:])
+        tanh_warmer = sbuf.tile([P, 1], F32)
+        nc.scalar.activation(out=tanh_warmer[:], in_=two_eps[:], func=ACT.Tanh)
+        half_bias = sbuf.tile([P, BLOCKS], F32)
+        nc.scalar.activation(out=half_bias[:], in_=bias_ps[:, 0:BLOCKS], func=ACT.Copy, scale=0.5)
         grouped = [sbuf.tile([P, 4 * P], BF16, align_bytes=64, name="grouped%d" % g) for g in range(PASSES)]
         codes = [sbuf.tile([P, P], U32, align_bytes=64, name="codes%d" % g) for g in range(PASSES)]
         act_planes = [sbuf.tile([P, P], U8, align_bytes=64, name="act_plane%d" % g) for g in range(PASSES)]
@@ -130,16 +135,22 @@ def tile_slstmcell_pb_s_kernel(
         def quantise(g):
             nc.vector.quantize_mx(out=codes[g][:].bitcast(FP8X4), scales=act_planes[g][:], in_=grouped[g][:])
 
+        half_recip = sbuf.tile([P, D_H], F32)
+        ratio = sbuf.tile([P, D_H], F32)
+
+        def square_root(cols):
+            nc.vector.tensor_tensor(out=half_recip[:, cols], in0=root[:, cols], in1=root[:, cols], op=ALU.mult)
+
         regroup(1)
         regroup(2)
         quantise(1)
         quantise(2)
         regroup(0)
+        square_root(halves[0])
         quantise(0)
-        c_root = sbuf.tile([P, D_H], F32)
-        ratio = sbuf.tile([P, D_H], F32)
+        square_root(halves[1])
         for cols in halves:
-            nc.vector.tensor_tensor(out=c_root[:, cols], in0=c_sb[:, cols], in1=root[:, cols], op=ALU.mult)
+            nc.vector.tensor_tensor(out=ratio[:, cols], in0=c_sb[:, cols], in1=half_recip[:, cols], op=ALU.mult)
 
         acc = {j: psum.tile([P, P], F32, name="acc%d" % j, tag="bank%d" % j) for j in range(HEAD)}
         th = [sbuf.tile([P, 2, P], F32, name="th%d" % i) for i in range(PAIRS)]
@@ -186,13 +197,6 @@ def tile_slstmcell_pb_s_kernel(
         for j in range(HEAD):
             multiply(j, 1)
             multiply(j, 2)
-
-        bias_ps = psum.tile([P, P], BF16, tag="bank7")
-        nc.tensor.transpose(bias_ps[:], bias_rows[:], ident_bf[:])
-        half_bias = sbuf.tile([P, BLOCKS], F32)
-        nc.vector.tensor_scalar(out=half_bias[:], in0=bias_ps[:, 0:BLOCKS], scalar1=0.5, scalar2=None, op0=ALU.mult)
-        for cols in halves:
-            nc.vector.tensor_tensor(out=ratio[:, cols], in0=c_root[:, cols], in1=root[:, cols], op=ALU.mult)
 
         for j in range(HEAD):
             multiply(j, 0)

@@ -21,8 +21,6 @@ PASSES = (D_IN + D_H) // K_PASS
 BLOCKS = D_H // P
 HALF = D_H // 2
 PAIRS = BLOCKS // 2
-ORDER = (1, 2, 0)
-HEAD = 6
 EPS = 1e-6
 
 FLOPS = 2 * P * (D_IN + D_H) * D_H
@@ -46,8 +44,8 @@ def tile_slstmcell_pb_s_kernel(
         stack.enter_context(tc.manual_schedule())
         halves = [slice(k * HALF, (k + 1) * HALF) for k in range(2)]
 
-        bias_rows = sbuf.tile([P, P], BF16)
-        nc.vector.memset(bias_rows[:], 0.0)
+        w_planes = sbuf.tile([P, 1, D_H], U8, align_bytes=64)
+        nc.vector.memset(w_planes[:].bitcast(I32), 0)
         idle_in = sbuf.tile([P, 2 * P], F32)
         nc.vector.memset(idle_in[:], 1.0)
         two_eps = sbuf.tile([P, 1], F32)
@@ -56,8 +54,8 @@ def tile_slstmcell_pb_s_kernel(
         nc.scalar.activation(out=table_warmer[:], in_=two_eps[:], func=ACT.Abs_reciprocal_sqrt)
         u_planes = sbuf.tile([P, 2, D_H], U8, align_bytes=64)
         nc.vector.memset(u_planes[:].bitcast(I32), 0)
-        w_planes = sbuf.tile([P, 1, D_H], U8, align_bytes=64)
-        nc.vector.memset(w_planes[:].bitcast(I32), 0)
+        bias_rows = sbuf.tile([P, P], BF16)
+        nc.vector.memset(bias_rows[:], 0.0)
         planes = [w_planes[:, 0, :], u_planes[:, 0, :], u_planes[:, 1, :]]
 
         c_sb = sbuf.tile([P, D_H], BF16)
@@ -65,27 +63,26 @@ def tile_slstmcell_pb_s_kernel(
         ident = sbuf.tile([P, P], F32)
         make_identity(nc, ident[:])
 
-        acts = sbuf.tile([P, PASSES, K_PASS], BF16)
-        nc.sync.dma_start(out=acts[:, 1:3, :], in_=h_prev.rearrange("b (g k) -> b g k", g=2))
+        x_sb = sbuf.tile([P, D_IN], BF16)
+        nc.sync.dma_start(out=x_sb[:], in_=x)
         n_sb = sbuf.tile([P, D_H], BF16)
         nc.sync.dma_start(out=n_sb[:], in_=n)
-        nc.sync.dma_start(out=acts[:, 0, :], in_=x)
+        load_scale_rows(nc, w_planes, W_o_scales)
+        h_sb = sbuf.tile([P, D_H], BF16)
+        nc.sync.dma_start(out=h_sb[:], in_=h_prev)
+        w_words = sbuf.tile([P, 2 * D_H], U8, align_bytes=64)
+        nc.sync.dma_start(out=w_words[:].bitcast(I32), in_=W_o_words[0].bitcast(I32))
         load_scale_rows(nc, u_planes, U_o_scales)
-        cuts = ((0, HEAD), (HEAD, BLOCKS))
-        u_words = [sbuf.tile([P, 2, 2 * P * (b - a)], U8, align_bytes=64, name="u_words%d" % a) for a, b in cuts]
+        u_words = [sbuf.tile([P, 2, 2 * HALF], U8, align_bytes=64, name="u_words%d" % k) for k in range(2)]
 
         def load_u(k):
-            a, b = cuts[k]
             nc.sync.dma_start(
                 out=u_words[k][:].bitcast(I32),
-                in_=U_o_words[:, :, 2 * P * a : 2 * P * b].rearrange("g p w -> p g w").bitcast(I32),
+                in_=U_o_words[:, :, 2 * HALF * k : 2 * HALF * (k + 1)].rearrange("g p w -> p g w").bitcast(I32),
             )
 
         load_u(0)
         nc.sync.dma_start(out=bias_rows[0:BLOCKS, :], in_=b_o.rearrange("(j p) -> j p", p=P))
-        w_words = sbuf.tile([P, 2 * D_H], U8, align_bytes=64)
-        nc.sync.dma_start(out=w_words[:].bitcast(I32), in_=W_o_words[0].bitcast(I32))
-        load_scale_rows(nc, w_planes, W_o_scales)
         load_u(1)
 
         root = sbuf.tile([P, D_H], F32)
@@ -94,7 +91,7 @@ def tile_slstmcell_pb_s_kernel(
                 out=root[:, cols], in_=n_sb[:, cols], func=ACT.Abs_reciprocal_sqrt, bias=two_eps[:, 0:1], scale=2.0
             )
 
-        idle_out = psum.tile([P, 2 * P], F32, tag="bank5")
+        idle_out = psum.tile([P, 2 * P], F32, tag="bank4")
 
         def keep_warm(width):
             nc.tensor.matmul(out=idle_out[:, 0:width], lhsT=idle_in[:, 0:P], rhs=idle_in[:, 0:width], start=True, stop=True)
@@ -102,26 +99,23 @@ def tile_slstmcell_pb_s_kernel(
         keep_warm(2 * P)
         keep_warm(P)
 
-        flipped = [psum.tile([P, 2, P], F32, name="flipped%d" % b, tag="bank%d" % b) for b in (7, 0, 1)]
+        ident_bf = sbuf.tile([P, P], BF16)
+        nc.vector.tensor_copy(out=ident_bf[:], in_=ident[:])
+
+        acts = (x_sb[:], h_sb[:, 0:K_PASS], h_sb[:, K_PASS : 2 * K_PASS])
+        flipped = [psum.tile([P, 2, P], F32, name="flipped%d" % b, tag="bank%d" % b) for b in (0, 5, 6)]
 
         def flip(g):
-            pair_words = acts[:, g, :].bitcast(F32)
+            pair_words = acts[g].bitcast(F32)
             for u in range(2):
                 nc.tensor.transpose(flipped[g][:, u, :], pair_words[:, u : K_PASS // 2 : 2], ident[:])
 
+        flip(0)
+        keep_warm(P)
         flip(1)
         flip(2)
-        flip(0)
-        keep_warm(2 * P)
+        keep_warm(P)
 
-        ident_bf = sbuf.tile([P, P], BF16)
-        nc.vector.tensor_copy(out=ident_bf[:], in_=ident[:])
-        bias_ps = psum.tile([P, P], BF16, tag="bank6")
-        nc.tensor.transpose(bias_ps[:], bias_rows[:], ident_bf[:])
-        tanh_warmer = sbuf.tile([P, 1], F32)
-        nc.scalar.activation(out=tanh_warmer[:], in_=two_eps[:], func=ACT.Tanh)
-        half_bias = sbuf.tile([P, BLOCKS], F32)
-        nc.scalar.activation(out=half_bias[:], in_=bias_ps[:, 0:BLOCKS], func=ACT.Copy, scale=0.5)
         grouped = [sbuf.tile([P, 4 * P], BF16, align_bytes=64, name="grouped%d" % g) for g in range(PASSES)]
         codes = [sbuf.tile([P, P], U32, align_bytes=64, name="codes%d" % g) for g in range(PASSES)]
         act_planes = [sbuf.tile([P, P], U8, align_bytes=64, name="act_plane%d" % g) for g in range(PASSES)]
@@ -138,29 +132,25 @@ def tile_slstmcell_pb_s_kernel(
         half_recip = sbuf.tile([P, D_H], F32)
         ratio = sbuf.tile([P, D_H], F32)
 
-        def square_root(cols):
-            nc.vector.tensor_tensor(out=half_recip[:, cols], in0=root[:, cols], in1=root[:, cols], op=ALU.mult)
-
+        regroup(0)
+        quantise(0)
         regroup(1)
         regroup(2)
         quantise(1)
         quantise(2)
-        regroup(0)
-        square_root(halves[0])
-        quantise(0)
-        square_root(halves[1])
+        for cols in halves:
+            nc.vector.tensor_tensor(out=half_recip[:, cols], in0=root[:, cols], in1=root[:, cols], op=ALU.mult)
         for cols in halves:
             nc.vector.tensor_tensor(out=ratio[:, cols], in0=c_sb[:, cols], in1=half_recip[:, cols], op=ALU.mult)
 
-        acc = {j: psum.tile([P, P], F32, name="acc%d" % j, tag="bank%d" % j) for j in range(HEAD)}
+        acc = {j: psum.tile([P, P], F32, name="acc%d" % j, tag="bank%d" % j) for j in range(BLOCKS - 1)}
         th = [sbuf.tile([P, 2, P], F32, name="th%d" % i) for i in range(PAIRS)]
 
         def multiply(j, g):
             if g == 0:
                 words = w_words[:, 2 * P * j : 2 * P * (j + 1)]
             else:
-                k = int(j >= HEAD)
-                i = j - cuts[k][0]
+                k, i = divmod(j, BLOCKS // 2)
                 words = u_words[k][:, g - 1, 2 * P * i : 2 * P * (i + 1)]
             nc.tensor.matmul_mx(
                 out=acc[j][:],
@@ -168,8 +158,8 @@ def tile_slstmcell_pb_s_kernel(
                 lhsT_scale=planes[g][:, P * j : P * (j + 1)],
                 rhs=codes[g][:].bitcast(FP8X4),
                 rhs_scale=act_planes[g][:],
-                start=(g == ORDER[0]),
-                stop=(g == ORDER[-1]),
+                start=(g == 0),
+                stop=(g == PASSES - 1),
             )
 
         def gate(j):
@@ -194,19 +184,22 @@ def tile_slstmcell_pb_s_kernel(
             )
             nc.sync.dma_start(out=out[:, cols], in_=h_new[:, cols])
 
-        for j in range(HEAD):
-            multiply(j, 1)
-            multiply(j, 2)
+        for j in range(BLOCKS - 1):
+            multiply(j, 0)
 
-        for j in range(HEAD):
-            multiply(j, 0)
-            gate(j)
-        for j in range(HEAD, BLOCKS):
-            acc[j] = psum.tile([P, P], F32, name="acc%d" % j, tag="bank%d" % j)
+        bias_ps = psum.tile([P, P], BF16, tag="bank7")
+        nc.tensor.transpose(bias_ps[:], bias_rows[:], ident_bf[:])
+        tanh_warmer = sbuf.tile([P, 1], F32)
+        nc.scalar.activation(out=tanh_warmer[:], in_=two_eps[:], func=ACT.Tanh)
+        half_bias = sbuf.tile([P, BLOCKS], F32)
+        nc.scalar.activation(out=half_bias[:], in_=bias_ps[:, 0:BLOCKS], func=ACT.Copy, scale=0.5)
+
+        acc[7] = psum.tile([P, P], F32, name="acc7", tag="bank7")
+        for j in range(BLOCKS):
+            if j == 7:
+                multiply(j, 0)
             multiply(j, 1)
             multiply(j, 2)
-        for j in range(HEAD, BLOCKS):
-            multiply(j, 0)
             gate(j)
         for i in range(PAIRS):
             finish(i)

@@ -58,8 +58,6 @@ def tile_slstmcell_pb_s_kernel(
         nc.vector.memset(bias_rows[:], 0.0)
         planes = [w_planes[:, 0, :], u_planes[:, 0, :], u_planes[:, 1, :]]
 
-        c_sb = sbuf.tile([P, D_H], BF16)
-        nc.gpsimd.dma_start(out=c_sb[:], in_=c)
         ident = sbuf.tile([P, P], F32)
         make_identity(nc, ident[:])
 
@@ -67,12 +65,11 @@ def tile_slstmcell_pb_s_kernel(
         nc.sync.dma_start(out=x_sb[:], in_=x)
         n_sb = sbuf.tile([P, D_H], BF16)
         nc.sync.dma_start(out=n_sb[:], in_=n)
-        load_scale_rows(nc, w_planes, W_o_scales)
         h_sb = sbuf.tile([P, D_H], BF16)
         nc.sync.dma_start(out=h_sb[:], in_=h_prev)
+        load_scale_rows(nc, w_planes, W_o_scales)
         w_words = sbuf.tile([P, 2 * D_H], U8, align_bytes=64)
         nc.sync.dma_start(out=w_words[:].bitcast(I32), in_=W_o_words[0].bitcast(I32))
-        load_scale_rows(nc, u_planes, U_o_scales)
         u_words = [sbuf.tile([P, 2, 2 * HALF], U8, align_bytes=64, name="u_words%d" % k) for k in range(2)]
 
         def load_u(k):
@@ -82,8 +79,12 @@ def tile_slstmcell_pb_s_kernel(
             )
 
         load_u(0)
+        load_scale_rows(nc, u_planes, U_o_scales)
         nc.sync.dma_start(out=bias_rows[0:BLOCKS, :], in_=b_o.rearrange("(j p) -> j p", p=P))
         load_u(1)
+        c_sb = sbuf.tile([P, D_H], BF16)
+        for cols in halves:
+            nc.sync.dma_start(out=c_sb[:, cols], in_=c[:, cols])
 
         root = sbuf.tile([P, D_H], F32)
         for cols in halves:

@@ -60,6 +60,7 @@ def tile_slstmcell_pb_s_kernel(
 
         ident = sbuf.tile([P, P], F32)
         make_identity(nc, ident[:])
+        nc.gpsimd.dma_start(out=bias_rows[0:BLOCKS, :], in_=b_o.rearrange("(j p) -> j p", p=P))
 
         x_sb = sbuf.tile([P, D_IN], BF16)
         nc.sync.dma_start(out=x_sb[:], in_=x)
@@ -80,7 +81,6 @@ def tile_slstmcell_pb_s_kernel(
 
         load_u(0)
         load_scale_rows(nc, u_planes, U_o_scales)
-        nc.sync.dma_start(out=bias_rows[0:BLOCKS, :], in_=b_o.rearrange("(j p) -> j p", p=P))
         load_u(1)
         c_sb = sbuf.tile([P, D_H], BF16)
         for cols in halves:
@@ -139,10 +139,10 @@ def tile_slstmcell_pb_s_kernel(
         regroup(2)
         quantise(1)
         quantise(2)
-        for cols in halves:
+
+        def square(k):
+            cols = halves[k]
             nc.vector.tensor_tensor(out=half_recip[:, cols], in0=root[:, cols], in1=root[:, cols], op=ALU.mult)
-        for cols in halves:
-            nc.vector.tensor_tensor(out=ratio[:, cols], in0=c_sb[:, cols], in1=half_recip[:, cols], op=ALU.mult)
 
         acc = {j: psum.tile([P, P], F32, name="acc%d" % j, tag="bank%d" % j) for j in range(BLOCKS - 1)}
         th = [sbuf.tile([P, 2, P], F32, name="th%d" % i) for i in range(PAIRS)]
@@ -190,10 +190,16 @@ def tile_slstmcell_pb_s_kernel(
 
         bias_ps = psum.tile([P, P], BF16, tag="bank7")
         nc.tensor.transpose(bias_ps[:], bias_rows[:], ident_bf[:])
+        half_bias = sbuf.tile([P, BLOCKS], F32)
+        square(0)
+        nc.vector.tensor_scalar(
+            out=half_bias[:], in0=bias_ps[:, 0:BLOCKS], scalar1=0.5, scalar2=None, op0=ALU.mult
+        )
+        square(1)
+        for cols in halves:
+            nc.vector.tensor_tensor(out=ratio[:, cols], in0=c_sb[:, cols], in1=half_recip[:, cols], op=ALU.mult)
         tanh_warmer = sbuf.tile([P, 1], F32)
         nc.scalar.activation(out=tanh_warmer[:], in_=two_eps[:], func=ACT.Tanh)
-        half_bias = sbuf.tile([P, BLOCKS], F32)
-        nc.scalar.activation(out=half_bias[:], in_=bias_ps[:, 0:BLOCKS], func=ACT.Copy, scale=0.5)
 
         acc[7] = psum.tile([P, P], F32, name="acc7", tag="bank7")
         for j in range(BLOCKS):

@@ -45,7 +45,7 @@ def tile_slstmcell_pb_s_kernel(
         halves = [slice(k * HALF, (k + 1) * HALF) for k in range(2)]
 
         w_planes = sbuf.tile([P, 1, D_H], U8, align_bytes=64)
-        nc.vector.memset(w_planes[:].bitcast(I32), 0)
+        nc.gpsimd.memset(w_planes[:].bitcast(I32), 0)
         idle_in = sbuf.tile([P, 2 * P], F32)
         nc.vector.memset(idle_in[:], 1.0)
         two_eps = sbuf.tile([P, 1], F32)
@@ -66,9 +66,9 @@ def tile_slstmcell_pb_s_kernel(
         nc.sync.dma_start(out=x_sb[:], in_=x)
         n_sb = sbuf.tile([P, D_H], BF16)
         nc.sync.dma_start(out=n_sb[:], in_=n)
+        load_scale_rows(nc, w_planes, W_o_scales)
         h_sb = sbuf.tile([P, D_H], BF16)
         nc.sync.dma_start(out=h_sb[:], in_=h_prev)
-        load_scale_rows(nc, w_planes, W_o_scales)
         w_words = sbuf.tile([P, 2 * D_H], U8, align_bytes=64)
         nc.sync.dma_start(out=w_words[:].bitcast(I32), in_=W_o_words[0].bitcast(I32))
         u_words = [sbuf.tile([P, 2, 2 * HALF], U8, align_bytes=64, name="u_words%d" % k) for k in range(2)]

@@ -55,7 +55,7 @@ def tile_slstmcell_pb_s_kernel(
         u_planes = sbuf.tile([P, 2, D_H], U8, align_bytes=64)
         nc.vector.memset(u_planes[:].bitcast(I32), 0)
         bias_rows = sbuf.tile([P, P], BF16)
-        nc.vector.memset(bias_rows[:], 0.0)
+        nc.gpsimd.memset(bias_rows[:], 0.0)
         planes = [w_planes[:, 0, :], u_planes[:, 0, :], u_planes[:, 1, :]]
 
         ident = sbuf.tile([P, P], F32)

@@ -98,7 +98,6 @@ def tile_slstmcell_pb_s_kernel(
             nc.tensor.matmul(out=idle_out[:, 0:width], lhsT=idle_in[:, 0:P], rhs=idle_in[:, 0:width], start=True, stop=True)
 
         keep_warm(2 * P)
-        keep_warm(P)
 
         ident_bf = sbuf.tile([P, P], BF16)
         nc.vector.tensor_copy(out=ident_bf[:], in_=ident[:])
@@ -112,7 +111,7 @@ def tile_slstmcell_pb_s_kernel(
                 nc.tensor.transpose(flipped[g][:, u, :], pair_words[:, u : K_PASS // 2 : 2], ident[:])
 
         flip(0)
-        keep_warm(P)
+        keep_warm(2 * P)
         flip(1)
         flip(2)
         keep_warm(P)
@@ -183,7 +182,8 @@ def tile_slstmcell_pb_s_kernel(
                 op0=ALU.add,
                 op1=ALU.mult,
             )
-            nc.sync.dma_start(out=out[:, cols], in_=h_new[:, cols])
+            queue = nc.scalar if i % 2 else nc.sync
+            queue.dma_start(out=out[:, cols], in_=h_new[:, cols])
 
         for j in range(BLOCKS - 1):
             multiply(j, 0)

from contextlib import ExitStack

import concourse.mybir as mybir
from concourse.masks import make_identity

F32 = mybir.dt.float32
BF16 = mybir.dt.bfloat16
I32 = mybir.dt.int32
U8 = mybir.dt.uint8
U32 = mybir.dt.uint32
FP8X4 = mybir.dt.float8_e4m3fn_x4
FP4X4 = mybir.dt.float4_e2m1fn_x4
ACT = mybir.ActivationFunctionType
ALU = mybir.AluOpType

P = 128
D_IN = 512
D_H = 1024
K_PASS = 512
PASSES = (D_IN + D_H) // K_PASS
BLOCKS = D_H // P
HALF = D_H // 2
PAIRS = BLOCKS // 2
EPS = 1e-6

FLOPS = 2 * P * (D_IN + D_H) * D_H


def load_scale_rows(nc, planes, scale_rows):
    for r in range(4):
        nc.sync.dma_start(
            out=planes[r:P:32].bitcast(I32),
            in_=scale_rows[:, r:16:4, :].rearrange("g q w -> q g w").bitcast(I32),
        )


def tile_slstmcell_pb_s_kernel(
    tc, x, h_prev, c, n, W_o_words, W_o_scales, b_o, U_o_words, U_o_scales, out
):
    nc = tc.nc
    with ExitStack() as stack:
        sbuf = stack.enter_context(tc.tile_pool(name="sbuf", bufs=1))
        psum = stack.enter_context(tc.psum_pool(name="psum", bufs=1))
        stack.enter_context(tc.manual_schedule())
        halves = [slice(k * HALF, (k + 1) * HALF) for k in range(2)]

        w_planes = sbuf.tile([P, 1, D_H], U8, align_bytes=64)
        nc.gpsimd.memset(w_planes[:].bitcast(I32), 0)
        idle_in = sbuf.tile([P, 2 * P], F32)
        nc.vector.memset(idle_in[:], 1.0)
        two_eps = sbuf.tile([P, 1], F32)
        nc.vector.memset(two_eps[:], 2.0 * EPS)
        table_warmer = sbuf.tile([P, 1], F32)
        nc.scalar.activation(out=table_warmer[:], in_=two_eps[:], func=ACT.Abs_reciprocal_sqrt)
        u_planes = sbuf.tile([P, 2, D_H], U8, align_bytes=64)
        nc.vector.memset(u_planes[:].bitcast(I32), 0)
        bias_rows = sbuf.tile([P, P], BF16)
        nc.gpsimd.memset(bias_rows[:], 0.0)
        planes = [w_planes[:, 0, :], u_planes[:, 0, :], u_planes[:, 1, :]]

        ident = sbuf.tile([P, P], F32)
        make_identity(nc, ident[:])
        nc.gpsimd.dma_start(out=bias_rows[0:BLOCKS, :], in_=b_o.rearrange("(j p) -> j p", p=P))

        x_sb = sbuf.tile([P, D_IN], BF16)
        nc.sync.dma_start(out=x_sb[:], in_=x)
        n_sb = sbuf.tile([P, D_H], BF16)
        nc.sync.dma_start(out=n_sb[:], in_=n)
        load_scale_rows(nc, w_planes, W_o_scales)
        h_sb = sbuf.tile([P, D_H], BF16)
        nc.sync.dma_start(out=h_sb[:], in_=h_prev)
        w_words = sbuf.tile([P, 2 * D_H], U8, align_bytes=64)
        nc.sync.dma_start(out=w_words[:].bitcast(I32), in_=W_o_words[0].bitcast(I32))
        u_words = [sbuf.tile([P, 2, 2 * HALF], U8, align_bytes=64, name="u_words%d" % k) for k in range(2)]

        def load_u(k):
            nc.sync.dma_start(
                out=u_words[k][:].bitcast(I32),
                in_=U_o_words[:, :, 2 * HALF * k : 2 * HALF * (k + 1)].rearrange("g p w -> p g w").bitcast(I32),
            )

        load_u(0)
        load_scale_rows(nc, u_planes, U_o_scales)
        load_u(1)
        c_sb = sbuf.tile([P, D_H], BF16)
        for cols in halves:
            nc.sync.dma_start(out=c_sb[:, cols], in_=c[:, cols])

        root = sbuf.tile([P, D_H], F32)
        for cols in halves:
            nc.scalar.activation(
                out=root[:, cols], in_=n_sb[:, cols], func=ACT.Abs_reciprocal_sqrt, bias=two_eps[:, 0:1], scale=2.0
            )

        idle_out = psum.tile([P, 2 * P], F32, tag="bank4")

        def keep_warm(width):
            nc.tensor.matmul(out=idle_out[:, 0:width], lhsT=idle_in[:, 0:P], rhs=idle_in[:, 0:width], start=True, stop=True)

        keep_warm(2 * P)

        ident_bf = sbuf.tile([P, P], BF16)
        nc.vector.tensor_copy(out=ident_bf[:], in_=ident[:])

        acts = (x_sb[:], h_sb[:, 0:K_PASS], h_sb[:, K_PASS : 2 * K_PASS])
        flipped = [psum.tile([P, 2, P], F32, name="flipped%d" % b, tag="bank%d" % b) for b in (0, 5, 6)]

        def flip(g):
            pair_words = acts[g].bitcast(F32)
            for u in range(2):
                nc.tensor.transpose(flipped[g][:, u, :], pair_words[:, u : K_PASS // 2 : 2], ident[:])

        flip(0)
        keep_warm(2 * P)
        flip(1)
        flip(2)
        keep_warm(P)

        grouped = [sbuf.tile([P, 4 * P], BF16, align_bytes=64, name="grouped%d" % g) for g in range(PASSES)]
        codes = [sbuf.tile([P, P], U32, align_bytes=64, name="codes%d" % g) for g in range(PASSES)]
        act_planes = [sbuf.tile([P, P], U8, align_bytes=64, name="act_plane%d" % g) for g in range(PASSES)]

        def regroup(g):
            nc.vector.tensor_copy(
                out=grouped[g][:].bitcast(F32).rearrange("p (b u) -> p b u", u=2),
                in_=flipped[g][:].rearrange("p u b -> p b u"),
            )

        def quantise(g):
            nc.vector.quantize_mx(out=codes[g][:].bitcast(FP8X4), scales=act_planes[g][:], in_=grouped[g][:])

        half_recip = sbuf.tile([P, D_H], F32)
        ratio = sbuf.tile([P, D_H], F32)

        regroup(0)
        quantise(0)
        regroup(1)
        regroup(2)
        quantise(1)
        quantise(2)

        def square(k):
            cols = halves[k]
            nc.vector.tensor_tensor(out=half_recip[:, cols], in0=root[:, cols], in1=root[:, cols], op=ALU.mult)

        acc = {j: psum.tile([P, P], F32, name="acc%d" % j, tag="bank%d" % j) for j in range(BLOCKS - 1)}
        th = [sbuf.tile([P, 2, P], F32, name="th%d" % i) for i in range(PAIRS)]

        def multiply(j, g):
            if g == 0:
                words = w_words[:, 2 * P * j : 2 * P * (j + 1)]
            else:
                k, i = divmod(j, BLOCKS // 2)
                words = u_words[k][:, g - 1, 2 * P * i : 2 * P * (i + 1)]
            nc.tensor.matmul_mx(
                out=acc[j][:],
                lhsT=words.bitcast(FP4X4),
                lhsT_scale=planes[g][:, P * j : P * (j + 1)],
                rhs=codes[g][:].bitcast(FP8X4),
                rhs_scale=act_planes[g][:],
                start=(g == 0),
                stop=(g == PASSES - 1),
            )

        def gate(j):
            nc.scalar.activation(
                out=th[j // 2][:, j % 2, :], in_=acc[j][:], func=ACT.Tanh, bias=half_bias[:, j : j + 1], scale=0.5
            )

        h_new = sbuf.tile([P, D_H], F32)

        def finish(i):
            cols = slice(2 * P * i, 2 * P * (i + 1))
            th_rows = psum.tile([P, 2, P], F32, name="th_rows%d" % i, tag="bank%d" % i)
            for j in range(2):
                nc.tensor.transpose(th_rows[:, j, :], th[i][:, j, :], ident[:])
            nc.vector.scalar_tensor_tensor(
                out=h_new[:, cols],
                in0=th_rows[:].rearrange("p j b -> p (j b)"),
                scalar=1.0,
                in1=ratio[:, cols],
                op0=ALU.add,
                op1=ALU.mult,
            )
            queue = nc.scalar if i % 2 else nc.sync
            queue.dma_start(out=out[:, cols], in_=h_new[:, cols])

        for j in range(BLOCKS - 1):
            multiply(j, 0)

        bias_ps = psum.tile([P, P], BF16, tag="bank7")
        nc.tensor.transpose(bias_ps[:], bias_rows[:], ident_bf[:])
        half_bias = sbuf.tile([P, BLOCKS], F32)
        square(0)
        nc.vector.tensor_scalar(
            out=half_bias[:], in0=bias_ps[:, 0:BLOCKS], scalar1=0.5, scalar2=None, op0=ALU.mult
        )
        square(1)
        for cols in halves:
            nc.vector.tensor_tensor(out=ratio[:, cols], in0=c_sb[:, cols], in1=half_recip[:, cols], op=ALU.mult)
        tanh_warmer = sbuf.tile([P, 1], F32)
        nc.scalar.activation(out=tanh_warmer[:], in_=two_eps[:], func=ACT.Tanh)

        acc[7] = psum.tile([P, P], F32, name="acc7", tag="bank7")
        for j in range(BLOCKS):
            if j == 7:
                multiply(j, 0)
            multiply(j, 1)
            multiply(j, 2)
            gate(j)
        for i in range(PAIRS):
            finish(i)
